import numpy as np
import ml_dtypes


def mxq(x, axis, fmt="e4m3"):
    dtype, down = {"e4m3": (ml_dtypes.float8_e4m3fn, 7), "e5m2": (ml_dtypes.float8_e5m2, 14)}[fmt]
    v = np.moveaxis(np.asarray(x, np.float32).astype(ml_dtypes.bfloat16).astype(np.float64), axis, -1)
    blocks = v.reshape(v.shape[:-1] + (-1, 32))
    amax = np.abs(blocks).max(-1, keepdims=True)
    byte = np.maximum(np.where(amax > 0, np.frexp(amax)[1] - 1 + 127, 0) - down, 1)
    scale = np.exp2(byte - 127.0)
    codes = (blocks / scale).astype(np.float32).astype(dtype).astype(np.float64)
    return np.moveaxis((codes * scale).reshape(v.shape), -1, axis)


WIDE = False


def mx_kscale(k):
    if not WIDE:
        return np.ones(k)
    levels = np.array([10, -10, 5, -5, 0])
    a = np.random.permutation(np.resize(levels, k // 512 * 4)).reshape(k // 512, 4)
    idx = np.arange(k)
    return np.exp2(a[idx // 512, idx % 128 // 32])


BF16 = ml_dtypes.bfloat16


def bf(x):
    return np.asarray(x, np.float32).astype(BF16)


def f64(x):
    return np.asarray(x).astype(np.float64)


B, H, HKV, S, D = 1, 4, 2, 512, 128
G = H // HKV
NEG = -1e9


def setup_inputs():
    s = mx_kscale(S)
    keep = np.random.random((B, 1, S, S)) < 0.75
    return {"query": bf(np.random.standard_normal((B, H, S, D))),
            "key": bf(np.random.standard_normal((B, HKV, S, D))),
            "value": bf(np.random.standard_normal((B, HKV, S, D)) * 0.25 * np.sqrt(S) * s.max() / s[:, None]),
            "attention_mask": bf(np.where(keep, 0.5 * np.random.standard_normal((B, 1, S, S)) + np.log(s), NEG)),
            "sinks": bf(np.log(S * s.max()) - 3.5 + np.random.standard_normal(H))}


def reference(query, key, value, attention_mask, sinks):
    scaling = 1.0 / np.sqrt(D)
    k = np.repeat(f64(key), G, axis=1)
    attn = (f64(query) @ k.transpose(0, 1, 3, 2)) * scaling
    attn = attn + f64(attention_mask)[:, :, :, :attn.shape[-1]]
    sink_col = np.broadcast_to(f64(sinks).reshape(1, H, 1, 1), (B, H, S, 1))
    combined = np.concatenate([attn, sink_col], axis=-1)
    combined = combined - combined.max(-1, keepdims=True)
    e = np.exp(combined[..., :-1])
    den = e.sum(-1, keepdims=True) + np.exp(combined[..., -1:])
    eg = e.reshape(B, HKV, G * S, S)
    pv = mxq(eg, 3, "e4m3") @ mxq(f64(value), 2, "e4m3")
    out = pv.reshape(B, H, S, D) / den
    return out.transpose(0, 2, 1, 3)

@@ -1,0 +1,210 @@
+import math
+from contextlib import ExitStack
+
+import concourse.mybir as mybir
+from concourse.masks import make_identity
+
+BF16 = mybir.dt.bfloat16
+F32 = mybir.dt.float32
+U32 = mybir.dt.uint32
+U8 = mybir.dt.uint8
+FP8X4 = mybir.dt.float8_e4m3fn_x4
+ALU = mybir.AluOpType
+EXP = mybir.ActivationFunctionType.Exp
+
+P = 128
+PACK = 4
+HEADS = 4
+KV_HEADS = 2
+GROUP = HEADS // KV_HEADS
+SEQ = 512
+HEAD_DIM = 128
+Q_TILES = SEQ // P
+K_TILES = SEQ // P
+UNITS = Q_TILES * HEADS
+SCALING = 1.0 / math.sqrt(HEAD_DIM)
+
+FLOPS = 2 * 2 * HEADS * SEQ * SEQ * HEAD_DIM
+
+
+def tile_deepseekv4attention_s_kernel(tc, query, key, value, attention_mask, sinks, out):
+    nc = tc.nc
+
+    q_dram = [query[0, h].rearrange("(p r) d -> p r d", r=Q_TILES) for h in range(HEADS)]
+    mask_dram = attention_mask[0, 0].rearrange("(p r) k -> p r k", r=Q_TILES)
+    out_dram = out[0].rearrange("(p r) h d -> r p (h d)", r=Q_TILES)
+    k_dram = [key[0, g].rearrange("(t p) d -> p t d", p=P) for g in range(KV_HEADS)]
+    v_dram = value[0].rearrange("g (t p) d -> p g t d", p=P)
+
+    with ExitStack() as ctx:
+        ctx.enter_context(tc.manual_schedule())
+        keep = ctx.enter_context(tc.tile_pool(name="keep", bufs=1))
+        work = ctx.enter_context(tc.tile_pool(name="work", bufs=3))
+        per_round = ctx.enter_context(tc.tile_pool(name="per_round", bufs=2))
+        score_banks = ctx.enter_context(tc.psum_pool(name="score_banks", bufs=3))
+        flip_banks = ctx.enter_context(tc.psum_pool(name="flip_banks", bufs=3))
+        product_banks = ctx.enter_context(tc.psum_pool(name="product_banks", bufs=2))
+
+        sinks_bf = keep.tile([P, HEADS], BF16)
+        nc.scalar.dma_start(out=sinks_bf[:], in_=sinks.partition_broadcast(P))
+        k_sb = [keep.tile([P, K_TILES, HEAD_DIM], BF16, name="k_sb%d" % g) for g in range(KV_HEADS)]
+        q_sb = [keep.tile([P, Q_TILES, HEAD_DIM], BF16, name="q_sb%d" % h) for h in range(HEADS)]
+        mask_sb = keep.tile([P, Q_TILES, SEQ], BF16)
+        v_sb = keep.tile([P, KV_HEADS, K_TILES, HEAD_DIM], BF16)
+        nc.sync.dma_start(out=k_sb[0][:], in_=k_dram[0])
+        for h in range(HEADS):
+            nc.sync.dma_start(out=q_sb[h][:], in_=q_dram[h])
+        nc.sync.dma_start(out=mask_sb[:, 0:1, :], in_=mask_dram[:, 0:1, :])
+        nc.sync.dma_start(out=k_sb[1][:], in_=k_dram[1])
+        nc.sync.dma_start(out=v_sb[:], in_=v_dram)
+        nc.sync.dma_start(out=mask_sb[:, 1:Q_TILES, :], in_=mask_dram[:, 1:Q_TILES, :])
+
+        identity = keep.tile([P, P], BF16)
+        make_identity(nc, identity[:])
+        zero = keep.tile([P, 1], F32)
+        one = keep.tile([P, 1], F32)
+        nc.vector.memset(zero[:], 0.0)
+        nc.scalar.activation(out=one[:], in_=zero[:], func=EXP)
+
+        s_sb = [keep.tile([P, SEQ + 1], F32, name="s_sb%d" % h) for h in range(HEADS)]
+        for h in range(HEADS):
+            nc.vector.tensor_copy(out=s_sb[h][:, SEQ : SEQ + 1], in_=sinks_bf[:, h : h + 1])
+
+        kT = [keep.tile([P, K_TILES, P], BF16, name="kT%d" % g) for g in range(KV_HEADS)]
+        qT = [keep.tile([P, HEADS, P], BF16, name="qT%d" % r) for r in range(Q_TILES)]
+        v_grouped = keep.tile([P, KV_HEADS, HEAD_DIM, PACK], BF16, align_bytes=64)
+        v_codes = keep.tile([P, KV_HEADS, HEAD_DIM], U32, align_bytes=64)
+        v_scales = keep.tile([P, KV_HEADS, HEAD_DIM], U8, align_bytes=64)
+
+        def transpose_keys(g, copy):
+            flipped = flip_banks.tile([P, K_TILES, P], BF16, tag="flipped")
+            for t in range(K_TILES):
+                nc.tensor.transpose(flipped[:, t, :], k_sb[g][:, t, :], identity[:])
+            copy(out=kT[g][:], in_=flipped[:])
+
+        def transpose_queries(r):
+            flipped = flip_banks.tile([P, HEADS, P], BF16, tag="flipped")
+            for h in range(HEADS):
+                nc.tensor.transpose(flipped[:, h, :], q_sb[h][:, r, :], identity[:])
+            nc.scalar.copy(out=qT[r][:], in_=flipped[:])
+
+        scores, neg_max, e_bf, e_flipped, e_grouped, e_codes, e_scales = {}, {}, {}, {}, {}, {}, {}
+        den, products = {}, {}
+
+        def multiply_qk(u):
+            r, h = divmod(u, HEADS)
+            scores[u] = score_banks.tile([P, SEQ], F32, name="scores")
+            nc.tensor.matmul(
+                out=scores[u][:],
+                lhsT=qT[r][:, h, :],
+                rhs=kT[h // GROUP][:].rearrange("d t p -> d (t p)"),
+                start=True,
+                stop=True,
+            )
+
+        def mask_and_max(u):
+            r, h = divmod(u, HEADS)
+            nc.vector.scalar_tensor_tensor(
+                out=s_sb[h][:, 0:SEQ],
+                in0=scores[u][:],
+                scalar=SCALING,
+                in1=mask_sb[:, r, :],
+                op0=ALU.mult,
+                op1=ALU.add,
+            )
+            neg_max[u] = work.tile([P, 1], F32, name="neg_max")
+            nc.vector.tensor_reduce(
+                out=neg_max[u][:], in_=s_sb[h][:], axis=mybir.AxisListType.X, op=ALU.max, negate=True
+            )
+
+        def exponentials(u):
+            r, h = divmod(u, HEADS)
+            if h == 0:
+                den[r] = per_round.tile([P, HEADS], F32, name="den")
+            e_bf[u] = work.tile([P, SEQ + 1], BF16, name="e_bf")
+            nc.scalar.activation(
+                out=e_bf[u][:],
+                in_=s_sb[h][:],
+                func=EXP,
+                bias=neg_max[u][:],
+                scale=1.0,
+                accum_out=den[r][:, h : h + 1],
+            )
+
+        def transpose_e(u):
+            e_flipped[u] = flip_banks.tile([P, PACK, P], BF16, name="e_flipped", tag="flipped")
+            for t in range(PACK):
+                nc.tensor.transpose(e_flipped[u][:, t, :], e_bf[u][:, t * P : (t + 1) * P], identity[:])
+
+        def group_e(u):
+            e_grouped[u] = work.tile([P, P, PACK], BF16, name="e_grouped", align_bytes=64)
+            nc.scalar.copy(out=e_grouped[u][:], in_=e_flipped[u][:].rearrange("p t q -> p q t"))
+
+        def quantise_e(u):
+            e_codes[u] = work.tile([P, P], U32, name="e_codes", align_bytes=64)
+            e_scales[u] = work.tile([P, P], U8, name="e_scales", align_bytes=64)
+            nc.vector.quantize_mx(
+                out=e_codes[u][:].bitcast(FP8X4),
+                scales=e_scales[u][:],
+                in_=e_grouped[u][:].rearrange("p q t -> p (q t)"),
+            )
+
+        def multiply_ev(u):
+            r, h = divmod(u, HEADS)
+            g = h // GROUP
+            if h == 0:
+                products[r] = product_banks.tile([P, HEADS, HEAD_DIM], F32, name="products")
+            nc.tensor.matmul_mx(
+                out=products[r][:, h, :],
+                lhsT=e_codes[u][:].bitcast(FP8X4),
+                lhsT_scale=e_scales[u][:],
+                rhs=v_codes[:, g, :].bitcast(FP8X4),
+                rhs_scale=v_scales[:, g, :],
+                start=True,
+                stop=True,
+            )
+
+        def divide_and_store(r):
+            inv_den = per_round.tile([P, HEADS], F32)
+            nc.vector.reciprocal(out=inv_den[:], in_=den[r][:])
+            result = per_round.tile([P, HEADS, HEAD_DIM], F32)
+            nc.vector.tensor_tensor(
+                out=result[:],
+                in0=products[r][:],
+                in1=inv_den[:].unsqueeze(2).to_broadcast([P, HEADS, HEAD_DIM]),
+                op=ALU.mult,
+            )
+            nc.sync.dma_start(out=out_dram[r], in_=result[:].rearrange("p h d -> p (h d)"))
+
+        transpose_keys(0, nc.vector.tensor_copy)
+        transpose_queries(0)
+        multiply_qk(0)
+        transpose_keys(1, nc.scalar.copy)
+
+        for n in range(UNITS + 4):
+            if n + 1 < UNITS:
+                multiply_qk(n + 1)
+            if 0 <= n - 2 < UNITS:
+                transpose_e(n - 2)
+            if 0 <= n - 4 < UNITS:
+                multiply_ev(n - 4)
+            if n % HEADS == 1 and n // HEADS + 1 < Q_TILES:
+                transpose_queries(n // HEADS + 1)
+            if 0 <= n - 3 < UNITS:
+                group_e(n - 3)
+            if 0 <= n - 1 < UNITS:
+                exponentials(n - 1)
+            if n == 0:
+                nc.scalar.copy(out=v_grouped[:], in_=v_sb[:].rearrange("p g t d -> p g d t"))
+            if n < UNITS:
+                mask_and_max(n)
+            if n == 1:
+                nc.vector.quantize_mx(
+                    out=v_codes[:].rearrange("p g d -> p (g d)").bitcast(FP8X4),
+                    scales=v_scales[:].rearrange("p g d -> p (g d)"),
+                    in_=v_grouped[:].rearrange("p g d t -> p (g d t)"),
+                )
+            if 0 <= n - 3 < UNITS:
+                quantise_e(n - 3)
+            if n >= 4 and (n - 4) % HEADS == HEADS - 1:
+                divide_and_store((n - 4) // HEADS)

@@ -10,10 +10,12 @@ U32 = mybir.dt.uint32
 U8 = mybir.dt.uint8
 FP8X4 = mybir.dt.float8_e4m3fn_x4
 ALU = mybir.AluOpType
-EXP = mybir.ActivationFunctionType.Exp
+ACT = mybir.ActivationFunctionType
 
 P = 128
 PACK = 4
+PAIR = 2
+HALVES = PACK // PAIR
 HEADS = 4
 KV_HEADS = 2
 GROUP = HEADS // KV_HEADS
@@ -34,7 +36,7 @@ def tile_deepseekv4attention_s_kernel(tc, query, key, value, attention_mask, sin
     mask_dram = attention_mask[0, 0].rearrange("(p r) k -> p r k", r=Q_TILES)
     out_dram = out[0].rearrange("(p r) h d -> r p (h d)", r=Q_TILES)
     k_dram = [key[0, g].rearrange("(t p) d -> p t d", p=P) for g in range(KV_HEADS)]
-    v_dram = value[0].rearrange("g (t p) d -> p g t d", p=P)
+    v_dram = value[0].rearrange("g (j p i) d -> p g j (i d)", j=HALVES, i=PAIR)
 
     with ExitStack() as ctx:
         ctx.enter_context(tc.manual_schedule())
@@ -42,67 +44,67 @@ def tile_deepseekv4attention_s_kernel(tc, query, key, value, attention_mask, sin
         work = ctx.enter_context(tc.tile_pool(name="work", bufs=3))
         per_round = ctx.enter_context(tc.tile_pool(name="per_round", bufs=2))
         score_banks = ctx.enter_context(tc.psum_pool(name="score_banks", bufs=3))
-        flip_banks = ctx.enter_context(tc.psum_pool(name="flip_banks", bufs=3))
-        product_banks = ctx.enter_context(tc.psum_pool(name="product_banks", bufs=2))
+        flip_banks = ctx.enter_context(tc.psum_pool(name="flip_banks", bufs=2))
+        product_banks = ctx.enter_context(tc.psum_pool(name="product_banks", bufs=3))
 
         sinks_bf = keep.tile([P, HEADS], BF16)
         nc.scalar.dma_start(out=sinks_bf[:], in_=sinks.partition_broadcast(P))
         k_sb = [keep.tile([P, K_TILES, HEAD_DIM], BF16, name="k_sb%d" % g) for g in range(KV_HEADS)]
         q_sb = [keep.tile([P, Q_TILES, HEAD_DIM], BF16, name="q_sb%d" % h) for h in range(HEADS)]
         mask_sb = keep.tile([P, Q_TILES, SEQ], BF16)
-        v_sb = keep.tile([P, KV_HEADS, K_TILES, HEAD_DIM], BF16)
+        v_sb = keep.tile([P, KV_HEADS, PACK, HEAD_DIM], BF16)
         nc.sync.dma_start(out=k_sb[0][:], in_=k_dram[0])
-        for h in range(HEADS):
-            nc.sync.dma_start(out=q_sb[h][:], in_=q_dram[h])
+        nc.sync.dma_start(out=q_sb[0][:], in_=q_dram[0])
         nc.sync.dma_start(out=mask_sb[:, 0:1, :], in_=mask_dram[:, 0:1, :])
+        nc.sync.dma_start(out=q_sb[1][:], in_=q_dram[1])
         nc.sync.dma_start(out=k_sb[1][:], in_=k_dram[1])
-        nc.sync.dma_start(out=v_sb[:], in_=v_dram)
+        nc.sync.dma_start(out=q_sb[2][:], in_=q_dram[2])
+        nc.sync.dma_start(out=q_sb[3][:], in_=q_dram[3])
+        nc.sync.dma_start(out=v_sb[:].rearrange("p g (j i) d -> p g j (i d)", i=PAIR), in_=v_dram)
         nc.sync.dma_start(out=mask_sb[:, 1:Q_TILES, :], in_=mask_dram[:, 1:Q_TILES, :])
 
-        identity = keep.tile([P, P], BF16)
-        make_identity(nc, identity[:])
+        identity_bf = keep.tile([P, P], BF16)
+        make_identity(nc, identity_bf[:])
+        identity_f32 = keep.tile([P, P], F32)
+        make_identity(nc, identity_f32[:])
         zero = keep.tile([P, 1], F32)
         one = keep.tile([P, 1], F32)
         nc.vector.memset(zero[:], 0.0)
-        nc.scalar.activation(out=one[:], in_=zero[:], func=EXP)
+        nc.scalar.activation(out=one[:], in_=zero[:], func=ACT.Exp)
 
         s_sb = [keep.tile([P, SEQ + 1], F32, name="s_sb%d" % h) for h in range(HEADS)]
         for h in range(HEADS):
             nc.vector.tensor_copy(out=s_sb[h][:, SEQ : SEQ + 1], in_=sinks_bf[:, h : h + 1])
 
         kT = [keep.tile([P, K_TILES, P], BF16, name="kT%d" % g) for g in range(KV_HEADS)]
-        qT = [keep.tile([P, HEADS, P], BF16, name="qT%d" % r) for r in range(Q_TILES)]
+        qT = [keep.tile([P, Q_TILES, P], BF16, name="qT%d" % h) for h in range(HEADS)]
         v_grouped = keep.tile([P, KV_HEADS, HEAD_DIM, PACK], BF16, align_bytes=64)
         v_codes = keep.tile([P, KV_HEADS, HEAD_DIM], U32, align_bytes=64)
         v_scales = keep.tile([P, KV_HEADS, HEAD_DIM], U8, align_bytes=64)
 
-        def transpose_keys(g, copy):
-            flipped = flip_banks.tile([P, K_TILES, P], BF16, tag="flipped")
-            for t in range(K_TILES):
-                nc.tensor.transpose(flipped[:, t, :], k_sb[g][:, t, :], identity[:])
-            copy(out=kT[g][:], in_=flipped[:])
+        def transpose_rows(rows_sb, rowsT, copy):
+            flipped = flip_banks.tile([P, SEQ // P, P], BF16, tag="flipped")
+            for c in range(SEQ // P):
+                nc.tensor.transpose(flipped[:, c, :], rows_sb[:, c, :], identity_bf[:])
+            copy(out=rowsT[:], in_=flipped[:])
 
-        def transpose_queries(r):
-            flipped = flip_banks.tile([P, HEADS, P], BF16, tag="flipped")
-            for h in range(HEADS):
-                nc.tensor.transpose(flipped[:, h, :], q_sb[h][:, r, :], identity[:])
-            nc.scalar.copy(out=qT[r][:], in_=flipped[:])
-
-        scores, neg_max, e_bf, e_flipped, e_grouped, e_codes, e_scales = {}, {}, {}, {}, {}, {}, {}
-        den, products = {}, {}
+        scores, neg_max, e_bf, e_flipped, e_grouped, e_codes, e_scales, product = (
+            {}, {}, {}, {}, {}, {}, {}, {},
+        )
+        den, inv_den, result = {}, {}, {}
 
         def multiply_qk(u):
             r, h = divmod(u, HEADS)
             scores[u] = score_banks.tile([P, SEQ], F32, name="scores")
             nc.tensor.matmul(
                 out=scores[u][:],
-                lhsT=qT[r][:, h, :],
+                lhsT=qT[h][:, r, :],
                 rhs=kT[h // GROUP][:].rearrange("d t p -> d (t p)"),
                 start=True,
                 stop=True,
             )
 
-        def mask_and_max(u):
+        def add_mask(u):
             r, h = divmod(u, HEADS)
             nc.vector.scalar_tensor_tensor(
                 out=s_sb[h][:, 0:SEQ],
@@ -112,6 +114,9 @@ def tile_deepseekv4attention_s_kernel(tc, query, key, value, attention_mask, sin
                 op0=ALU.mult,
                 op1=ALU.add,
             )
+
+        def negative_max(u):
+            h = u % HEADS
             neg_max[u] = work.tile([P, 1], F32, name="neg_max")
             nc.vector.tensor_reduce(
                 out=neg_max[u][:], in_=s_sb[h][:], axis=mybir.AxisListType.X, op=ALU.max, negate=True
@@ -121,24 +126,25 @@ def tile_deepseekv4attention_s_kernel(tc, query, key, value, attention_mask, sin
             r, h = divmod(u, HEADS)
             if h == 0:
                 den[r] = per_round.tile([P, HEADS], F32, name="den")
-            e_bf[u] = work.tile([P, SEQ + 1], BF16, name="e_bf")
+            e_bf[u] = work.tile([P, SEQ + PAIR], BF16, name="e_bf")
             nc.scalar.activation(
-                out=e_bf[u][:],
+                out=e_bf[u][:, 0 : SEQ + 1],
                 in_=s_sb[h][:],
-                func=EXP,
+                func=ACT.Exp,
                 bias=neg_max[u][:],
                 scale=1.0,
                 accum_out=den[r][:, h : h + 1],
             )
 
         def transpose_e(u):
-            e_flipped[u] = flip_banks.tile([P, PACK, P], BF16, name="e_flipped", tag="flipped")
-            for t in range(PACK):
-                nc.tensor.transpose(e_flipped[u][:, t, :], e_bf[u][:, t * P : (t + 1) * P], identity[:])
+            e_words = e_bf[u][:, 0:SEQ].bitcast(F32)
+            e_flipped[u] = flip_banks.tile([P, HALVES, P], F32, name="e_flipped", tag="flipped")
+            for j in range(HALVES):
+                nc.tensor.transpose(e_flipped[u][:, j, :], e_words[:, j * P : (j + 1) * P], identity_f32[:])
 
         def group_e(u):
-            e_grouped[u] = work.tile([P, P, PACK], BF16, name="e_grouped", align_bytes=64)
-            nc.scalar.copy(out=e_grouped[u][:], in_=e_flipped[u][:].rearrange("p t q -> p q t"))
+            e_grouped[u] = work.tile([P, P, HALVES], F32, name="e_grouped", align_bytes=64)
+            nc.scalar.copy(out=e_grouped[u][:], in_=e_flipped[u][:].rearrange("p j q -> p q j"))
 
         def quantise_e(u):
             e_codes[u] = work.tile([P, P], U32, name="e_codes", align_bytes=64)
@@ -146,16 +152,14 @@ def tile_deepseekv4attention_s_kernel(tc, query, key, value, attention_mask, sin
             nc.vector.quantize_mx(
                 out=e_codes[u][:].bitcast(FP8X4),
                 scales=e_scales[u][:],
-                in_=e_grouped[u][:].rearrange("p q t -> p (q t)"),
+                in_=e_grouped[u][:].rearrange("p q j -> p (q j)").bitcast(BF16),
             )
 
         def multiply_ev(u):
-            r, h = divmod(u, HEADS)
-            g = h // GROUP
-            if h == 0:
-                products[r] = product_banks.tile([P, HEADS, HEAD_DIM], F32, name="products")
+            g = (u % HEADS) // GROUP
+            product[u] = product_banks.tile([P, HEAD_DIM], F32, name="product")
             nc.tensor.matmul_mx(
-                out=products[r][:, h, :],
+                out=product[u][:],
                 lhsT=e_codes[u][:].bitcast(FP8X4),
                 lhsT_scale=e_scales[u][:],
                 rhs=v_codes[:, g, :].bitcast(FP8X4),
@@ -164,40 +168,48 @@ def tile_deepseekv4attention_s_kernel(tc, query, key, value, attention_mask, sin
                 stop=True,
             )
 
-        def divide_and_store(r):
-            inv_den = per_round.tile([P, HEADS], F32)
-            nc.vector.reciprocal(out=inv_den[:], in_=den[r][:])
-            result = per_round.tile([P, HEADS, HEAD_DIM], F32)
-            nc.vector.tensor_tensor(
-                out=result[:],
-                in0=products[r][:],
-                in1=inv_den[:].unsqueeze(2).to_broadcast([P, HEADS, HEAD_DIM]),
-                op=ALU.mult,
+        def invert_den(r):
+            inv_den[r] = per_round.tile([P, HEADS], F32, name="inv_den")
+            nc.vector.reciprocal(out=inv_den[r][:], in_=den[r][:])
+
+        def divide(u):
+            r, h = divmod(u, HEADS)
+            if h == 0:
+                result[r] = per_round.tile([P, HEADS, HEAD_DIM], F32, name="result")
+            nc.scalar.activation(
+                out=result[r][:, h, :], in_=product[u][:], func=ACT.Copy, scale=inv_den[r][:, h : h + 1]
             )
-            nc.sync.dma_start(out=out_dram[r], in_=result[:].rearrange("p h d -> p (h d)"))
+            if h == HEADS - 1:
+                nc.sync.dma_start(out=out_dram[r], in_=result[r][:].rearrange("p h d -> p (h d)"))
 
-        transpose_keys(0, nc.vector.tensor_copy)
-        transpose_queries(0)
+        transpose_rows(k_sb[0], kT[0], nc.vector.tensor_copy)
+        transpose_rows(q_sb[0], qT[0], nc.scalar.copy)
         multiply_qk(0)
-        transpose_keys(1, nc.scalar.copy)
+        transpose_rows(q_sb[1], qT[1], nc.scalar.copy)
+        multiply_qk(1)
+        add_mask(0)
+        transpose_rows(k_sb[1], kT[1], nc.scalar.copy)
+        transpose_rows(q_sb[2], qT[2], nc.scalar.copy)
+        transpose_rows(q_sb[3], qT[3], nc.scalar.copy)
+        nc.scalar.copy(out=v_grouped[:], in_=v_sb[:].rearrange("p g t d -> p g d t"))
 
-        for n in range(UNITS + 4):
-            if n + 1 < UNITS:
-                multiply_qk(n + 1)
+        for n in range(UNITS + 7):
+            if n + 2 < UNITS:
+                multiply_qk(n + 2)
             if 0 <= n - 2 < UNITS:
                 transpose_e(n - 2)
             if 0 <= n - 4 < UNITS:
                 multiply_ev(n - 4)
-            if n % HEADS == 1 and n // HEADS + 1 < Q_TILES:
-                transpose_queries(n // HEADS + 1)
             if 0 <= n - 3 < UNITS:
                 group_e(n - 3)
             if 0 <= n - 1 < UNITS:
                 exponentials(n - 1)
-            if n == 0:
-                nc.scalar.copy(out=v_grouped[:], in_=v_sb[:].rearrange("p g t d -> p g d t"))
+            if 0 <= n - 6 < UNITS:
+                divide(n - 6)
+            if n + 1 < UNITS:
+                add_mask(n + 1)
             if n < UNITS:
-                mask_and_max(n)
+                negative_max(n)
             if n == 1:
                 nc.vector.quantize_mx(
                     out=v_codes[:].rearrange("p g d -> p (g d)").bitcast(FP8X4),
@@ -206,5 +218,5 @@ def tile_deepseekv4attention_s_kernel(tc, query, key, value, attention_mask, sin
                 )
             if 0 <= n - 3 < UNITS:
                 quantise_e(n - 3)
-            if n >= 4 and (n - 4) % HEADS == HEADS - 1:
-                divide_and_store((n - 4) // HEADS)
+            if n >= 5 and (n - 5) % HEADS == 0 and (n - 5) // HEADS < Q_TILES:
+                invert_den((n - 5) // HEADS)

@@ -34,15 +34,15 @@ def tile_deepseekv4attention_s_kernel(tc, query, key, value, attention_mask, sin
 
     q_dram = [query[0, h].rearrange("(p r) d -> p r d", r=Q_TILES) for h in range(HEADS)]
     mask_dram = attention_mask[0, 0].rearrange("(p r) k -> p r k", r=Q_TILES)
-    out_dram = out[0].rearrange("(p r) h d -> r p (h d)", r=Q_TILES)
+    out_dram = out[0].rearrange("(p r) h d -> r h p d", r=Q_TILES)
     k_dram = [key[0, g].rearrange("(t p) d -> p t d", p=P) for g in range(KV_HEADS)]
     v_dram = value[0].rearrange("g (j p i) d -> p g j (i d)", j=HALVES, i=PAIR)
 
     with ExitStack() as ctx:
-        ctx.enter_context(tc.manual_schedule())
         keep = ctx.enter_context(tc.tile_pool(name="keep", bufs=1))
         work = ctx.enter_context(tc.tile_pool(name="work", bufs=3))
         per_round = ctx.enter_context(tc.tile_pool(name="per_round", bufs=2))
+        results = ctx.enter_context(tc.tile_pool(name="results", bufs=6))
         score_banks = ctx.enter_context(tc.psum_pool(name="score_banks", bufs=3))
         flip_banks = ctx.enter_context(tc.psum_pool(name="flip_banks", bufs=2))
         product_banks = ctx.enter_context(tc.psum_pool(name="product_banks", bufs=3))
@@ -55,12 +55,12 @@ def tile_deepseekv4attention_s_kernel(tc, query, key, value, attention_mask, sin
         v_sb = keep.tile([P, KV_HEADS, PACK, HEAD_DIM], BF16)
         nc.sync.dma_start(out=k_sb[0][:], in_=k_dram[0])
         nc.sync.dma_start(out=q_sb[0][:], in_=q_dram[0])
+        nc.sync.dma_start(out=v_sb[:].rearrange("p g (j i) d -> p g j (i d)", i=PAIR), in_=v_dram)
         nc.sync.dma_start(out=mask_sb[:, 0:1, :], in_=mask_dram[:, 0:1, :])
         nc.sync.dma_start(out=q_sb[1][:], in_=q_dram[1])
         nc.sync.dma_start(out=k_sb[1][:], in_=k_dram[1])
         nc.sync.dma_start(out=q_sb[2][:], in_=q_dram[2])
         nc.sync.dma_start(out=q_sb[3][:], in_=q_dram[3])
-        nc.sync.dma_start(out=v_sb[:].rearrange("p g (j i) d -> p g j (i d)", i=PAIR), in_=v_dram)
         nc.sync.dma_start(out=mask_sb[:, 1:Q_TILES, :], in_=mask_dram[:, 1:Q_TILES, :])
 
         identity_bf = keep.tile([P, P], BF16)
@@ -73,8 +73,6 @@ def tile_deepseekv4attention_s_kernel(tc, query, key, value, attention_mask, sin
         nc.scalar.activation(out=one[:], in_=zero[:], func=ACT.Exp)
 
         s_sb = [keep.tile([P, SEQ + 1], F32, name="s_sb%d" % h) for h in range(HEADS)]
-        for h in range(HEADS):
-            nc.vector.tensor_copy(out=s_sb[h][:, SEQ : SEQ + 1], in_=sinks_bf[:, h : h + 1])
 
         kT = [keep.tile([P, K_TILES, P], BF16, name="kT%d" % g) for g in range(KV_HEADS)]
         qT = [keep.tile([P, Q_TILES, P], BF16, name="qT%d" % h) for h in range(HEADS)]
@@ -91,7 +89,7 @@ def tile_deepseekv4attention_s_kernel(tc, query, key, value, attention_mask, sin
         scores, neg_max, e_bf, e_flipped, e_grouped, e_codes, e_scales, product = (
             {}, {}, {}, {}, {}, {}, {}, {},
         )
-        den, inv_den, result = {}, {}, {}
+        den, inv_den = {}, {}
 
         def multiply_qk(u):
             r, h = divmod(u, HEADS)
@@ -172,26 +170,31 @@ def tile_deepseekv4attention_s_kernel(tc, query, key, value, attention_mask, sin
             inv_den[r] = per_round.tile([P, HEADS], F32, name="inv_den")
             nc.vector.reciprocal(out=inv_den[r][:], in_=den[r][:])
 
-        def divide(u):
+        def divide_and_store(u):
             r, h = divmod(u, HEADS)
-            if h == 0:
-                result[r] = per_round.tile([P, HEADS, HEAD_DIM], F32, name="result")
+            result = results.tile([P, HEAD_DIM], F32)
             nc.scalar.activation(
-                out=result[r][:, h, :], in_=product[u][:], func=ACT.Copy, scale=inv_den[r][:, h : h + 1]
+                out=result[:], in_=product[u][:], func=ACT.Copy, scale=inv_den[r][:, h : h + 1]
             )
-            if h == HEADS - 1:
-                nc.sync.dma_start(out=out_dram[r], in_=result[r][:].rearrange("p h d -> p (h d)"))
+            nc.sync.dma_start(out=out_dram[r, h], in_=result[:])
 
         transpose_rows(k_sb[0], kT[0], nc.vector.tensor_copy)
         transpose_rows(q_sb[0], qT[0], nc.scalar.copy)
         multiply_qk(0)
+        nc.vector.tensor_copy(out=v_grouped[:], in_=v_sb[:].rearrange("p g t d -> p g d t"))
+        for h in range(HEADS):
+            nc.vector.tensor_copy(out=s_sb[h][:, SEQ : SEQ + 1], in_=sinks_bf[:, h : h + 1])
+        nc.vector.quantize_mx(
+            out=v_codes[:].rearrange("p g d -> p (g d)").bitcast(FP8X4),
+            scales=v_scales[:].rearrange("p g d -> p (g d)"),
+            in_=v_grouped[:].rearrange("p g d t -> p (g d t)"),
+        )
         transpose_rows(q_sb[1], qT[1], nc.scalar.copy)
         multiply_qk(1)
         add_mask(0)
         transpose_rows(k_sb[1], kT[1], nc.scalar.copy)
         transpose_rows(q_sb[2], qT[2], nc.scalar.copy)
         transpose_rows(q_sb[3], qT[3], nc.scalar.copy)
-        nc.scalar.copy(out=v_grouped[:], in_=v_sb[:].rearrange("p g t d -> p g d t"))
 
         for n in range(UNITS + 7):
             if n + 2 < UNITS:
@@ -205,17 +208,11 @@ def tile_deepseekv4attention_s_kernel(tc, query, key, value, attention_mask, sin
             if 0 <= n - 1 < UNITS:
                 exponentials(n - 1)
             if 0 <= n - 6 < UNITS:
-                divide(n - 6)
+                divide_and_store(n - 6)
             if n + 1 < UNITS:
                 add_mask(n + 1)
             if n < UNITS:
                 negative_max(n)
-            if n == 1:
-                nc.vector.quantize_mx(
-                    out=v_codes[:].rearrange("p g d -> p (g d)").bitcast(FP8X4),
-                    scales=v_scales[:].rearrange("p g d -> p (g d)"),
-                    in_=v_grouped[:].rearrange("p g d t -> p (g d t)"),
-                )
             if 0 <= n - 3 < UNITS:
                 quantise_e(n - 3)
             if n >= 5 and (n - 5) % HEADS == 0 and (n - 5) // HEADS < Q_TILES:

@@ -44,8 +44,8 @@ def tile_deepseekv4attention_s_kernel(tc, query, key, value, attention_mask, sin
         per_round = ctx.enter_context(tc.tile_pool(name="per_round", bufs=2))
         results = ctx.enter_context(tc.tile_pool(name="results", bufs=6))
         score_banks = ctx.enter_context(tc.psum_pool(name="score_banks", bufs=3))
-        flip_banks = ctx.enter_context(tc.psum_pool(name="flip_banks", bufs=2))
-        product_banks = ctx.enter_context(tc.psum_pool(name="product_banks", bufs=3))
+        flip_banks = ctx.enter_context(tc.psum_pool(name="flip_banks", bufs=3))
+        product_banks = ctx.enter_context(tc.psum_pool(name="product_banks", bufs=2))
 
         sinks_bf = keep.tile([P, HEADS], BF16)
         nc.scalar.dma_start(out=sinks_bf[:], in_=sinks.partition_broadcast(P))
@@ -73,6 +73,8 @@ def tile_deepseekv4attention_s_kernel(tc, query, key, value, attention_mask, sin
         nc.scalar.activation(out=one[:], in_=zero[:], func=ACT.Exp)
 
         s_sb = [keep.tile([P, SEQ + 1], F32, name="s_sb%d" % h) for h in range(HEADS)]
+        for h in range(HEADS):
+            nc.gpsimd.tensor_copy(out=s_sb[h][:, SEQ : SEQ + 1], in_=sinks_bf[:, h : h + 1])
 
         kT = [keep.tile([P, K_TILES, P], BF16, name="kT%d" % g) for g in range(KV_HEADS)]
         qT = [keep.tile([P, Q_TILES, P], BF16, name="qT%d" % h) for h in range(HEADS)]
@@ -154,10 +156,12 @@ def tile_deepseekv4attention_s_kernel(tc, query, key, value, attention_mask, sin
             )
 
         def multiply_ev(u):
-            g = (u % HEADS) // GROUP
-            product[u] = product_banks.tile([P, HEAD_DIM], F32, name="product")
+            r, h = divmod(u, HEADS)
+            g = h // GROUP
+            if h == 0:
+                product[r] = product_banks.tile([P, HEADS, HEAD_DIM], F32, name="product")
             nc.tensor.matmul_mx(
-                out=product[u][:],
+                out=product[r][:, h, :],
                 lhsT=e_codes[u][:].bitcast(FP8X4),
                 lhsT_scale=e_scales[u][:],
                 rhs=v_codes[:, g, :].bitcast(FP8X4),
@@ -174,46 +178,34 @@ def tile_deepseekv4attention_s_kernel(tc, query, key, value, attention_mask, sin
             r, h = divmod(u, HEADS)
             result = results.tile([P, HEAD_DIM], F32)
             nc.scalar.activation(
-                out=result[:], in_=product[u][:], func=ACT.Copy, scale=inv_den[r][:, h : h + 1]
+                out=result[:], in_=product[r][:, h, :], func=ACT.Copy, scale=inv_den[r][:, h : h + 1]
             )
             nc.sync.dma_start(out=out_dram[r, h], in_=result[:])
 
         transpose_rows(k_sb[0], kT[0], nc.vector.tensor_copy)
         transpose_rows(q_sb[0], qT[0], nc.scalar.copy)
-        multiply_qk(0)
         nc.vector.tensor_copy(out=v_grouped[:], in_=v_sb[:].rearrange("p g t d -> p g d t"))
-        for h in range(HEADS):
-            nc.vector.tensor_copy(out=s_sb[h][:, SEQ : SEQ + 1], in_=sinks_bf[:, h : h + 1])
         nc.vector.quantize_mx(
             out=v_codes[:].rearrange("p g d -> p (g d)").bitcast(FP8X4),
             scales=v_scales[:].rearrange("p g d -> p (g d)"),
             in_=v_grouped[:].rearrange("p g d t -> p (g d t)"),
         )
         transpose_rows(q_sb[1], qT[1], nc.scalar.copy)
-        multiply_qk(1)
-        add_mask(0)
         transpose_rows(k_sb[1], kT[1], nc.scalar.copy)
         transpose_rows(q_sb[2], qT[2], nc.scalar.copy)
         transpose_rows(q_sb[3], qT[3], nc.scalar.copy)
 
-        for n in range(UNITS + 7):
-            if n + 2 < UNITS:
-                multiply_qk(n + 2)
-            if 0 <= n - 2 < UNITS:
-                transpose_e(n - 2)
-            if 0 <= n - 4 < UNITS:
-                multiply_ev(n - 4)
-            if 0 <= n - 3 < UNITS:
-                group_e(n - 3)
-            if 0 <= n - 1 < UNITS:
-                exponentials(n - 1)
-            if 0 <= n - 6 < UNITS:
-                divide_and_store(n - 6)
-            if n + 1 < UNITS:
-                add_mask(n + 1)
-            if n < UNITS:
-                negative_max(n)
-            if 0 <= n - 3 < UNITS:
-                quantise_e(n - 3)
-            if n >= 5 and (n - 5) % HEADS == 0 and (n - 5) // HEADS < Q_TILES:
-                invert_den((n - 5) // HEADS)
+        for r in range(Q_TILES):
+            for h in range(HEADS):
+                u = r * HEADS + h
+                multiply_qk(u)
+                add_mask(u)
+                negative_max(u)
+                exponentials(u)
+                transpose_e(u)
+                group_e(u)
+                quantise_e(u)
+                multiply_ev(u)
+            invert_den(r)
+            for h in range(HEADS):
+                divide_and_store(r * HEADS + h)

import math
from contextlib import ExitStack

import concourse.mybir as mybir
from concourse.masks import make_identity

BF16 = mybir.dt.bfloat16
F32 = mybir.dt.float32
U32 = mybir.dt.uint32
U8 = mybir.dt.uint8
FP8X4 = mybir.dt.float8_e4m3fn_x4
ALU = mybir.AluOpType
ACT = mybir.ActivationFunctionType

P = 128
PACK = 4
PAIR = 2
HALVES = PACK // PAIR
HEADS = 4
KV_HEADS = 2
GROUP = HEADS // KV_HEADS
SEQ = 512
HEAD_DIM = 128
Q_TILES = SEQ // P
K_TILES = SEQ // P
UNITS = Q_TILES * HEADS
SCALING = 1.0 / math.sqrt(HEAD_DIM)

FLOPS = 2 * 2 * HEADS * SEQ * SEQ * HEAD_DIM


def tile_deepseekv4attention_s_kernel(tc, query, key, value, attention_mask, sinks, out):
    nc = tc.nc

    q_dram = [query[0, h].rearrange("(p r) d -> p r d", r=Q_TILES) for h in range(HEADS)]
    mask_dram = attention_mask[0, 0].rearrange("(p r) k -> p r k", r=Q_TILES)
    out_dram = out[0].rearrange("(p r) h d -> r h p d", r=Q_TILES)
    k_dram = [key[0, g].rearrange("(t p) d -> p t d", p=P) for g in range(KV_HEADS)]
    v_dram = value[0].rearrange("g (j p i) d -> p g j (i d)", j=HALVES, i=PAIR)

    with ExitStack() as ctx:
        keep = ctx.enter_context(tc.tile_pool(name="keep", bufs=1))
        work = ctx.enter_context(tc.tile_pool(name="work", bufs=3))
        per_round = ctx.enter_context(tc.tile_pool(name="per_round", bufs=2))
        results = ctx.enter_context(tc.tile_pool(name="results", bufs=6))
        score_banks = ctx.enter_context(tc.psum_pool(name="score_banks", bufs=3))
        flip_banks = ctx.enter_context(tc.psum_pool(name="flip_banks", bufs=3))
        product_banks = ctx.enter_context(tc.psum_pool(name="product_banks", bufs=2))

        sinks_bf = keep.tile([P, HEADS], BF16)
        nc.scalar.dma_start(out=sinks_bf[:], in_=sinks.partition_broadcast(P))
        k_sb = [keep.tile([P, K_TILES, HEAD_DIM], BF16, name="k_sb%d" % g) for g in range(KV_HEADS)]
        q_sb = [keep.tile([P, Q_TILES, HEAD_DIM], BF16, name="q_sb%d" % h) for h in range(HEADS)]
        mask_sb = keep.tile([P, Q_TILES, SEQ], BF16)
        v_sb = keep.tile([P, KV_HEADS, PACK, HEAD_DIM], BF16)
        nc.sync.dma_start(out=k_sb[0][:], in_=k_dram[0])
        nc.sync.dma_start(out=q_sb[0][:], in_=q_dram[0])
        nc.sync.dma_start(out=v_sb[:].rearrange("p g (j i) d -> p g j (i d)", i=PAIR), in_=v_dram)
        nc.sync.dma_start(out=mask_sb[:, 0:1, :], in_=mask_dram[:, 0:1, :])
        nc.sync.dma_start(out=q_sb[1][:], in_=q_dram[1])
        nc.sync.dma_start(out=k_sb[1][:], in_=k_dram[1])
        nc.sync.dma_start(out=q_sb[2][:], in_=q_dram[2])
        nc.sync.dma_start(out=q_sb[3][:], in_=q_dram[3])
        nc.sync.dma_start(out=mask_sb[:, 1:Q_TILES, :], in_=mask_dram[:, 1:Q_TILES, :])

        identity_bf = keep.tile([P, P], BF16)
        make_identity(nc, identity_bf[:])
        identity_f32 = keep.tile([P, P], F32)
        make_identity(nc, identity_f32[:])
        zero = keep.tile([P, 1], F32)
        one = keep.tile([P, 1], F32)
        nc.vector.memset(zero[:], 0.0)
        nc.scalar.activation(out=one[:], in_=zero[:], func=ACT.Exp)

        s_sb = [keep.tile([P, SEQ + 1], F32, name="s_sb%d" % h) for h in range(HEADS)]
        for h in range(HEADS):
            nc.gpsimd.tensor_copy(out=s_sb[h][:, SEQ : SEQ + 1], in_=sinks_bf[:, h : h + 1])

        kT = [keep.tile([P, K_TILES, P], BF16, name="kT%d" % g) for g in range(KV_HEADS)]
        qT = [keep.tile([P, Q_TILES, P], BF16, name="qT%d" % h) for h in range(HEADS)]
        v_grouped = keep.tile([P, KV_HEADS, HEAD_DIM, PACK], BF16, align_bytes=64)
        v_codes = keep.tile([P, KV_HEADS, HEAD_DIM], U32, align_bytes=64)
        v_scales = keep.tile([P, KV_HEADS, HEAD_DIM], U8, align_bytes=64)

        def transpose_rows(rows_sb, rowsT, copy):
            flipped = flip_banks.tile([P, SEQ // P, P], BF16, tag="flipped")
            for c in range(SEQ // P):
                nc.tensor.transpose(flipped[:, c, :], rows_sb[:, c, :], identity_bf[:])
            copy(out=rowsT[:], in_=flipped[:])

        scores, neg_max, e_bf, e_flipped, e_grouped, e_codes, e_scales, product = (
            {}, {}, {}, {}, {}, {}, {}, {},
        )
        den, inv_den = {}, {}

        def multiply_qk(u):
            r, h = divmod(u, HEADS)
            scores[u] = score_banks.tile([P, SEQ], F32, name="scores")
            nc.tensor.matmul(
                out=scores[u][:],
                lhsT=qT[h][:, r, :],
                rhs=kT[h // GROUP][:].rearrange("d t p -> d (t p)"),
                start=True,
                stop=True,
            )

        def add_mask(u):
            r, h = divmod(u, HEADS)
            nc.vector.scalar_tensor_tensor(
                out=s_sb[h][:, 0:SEQ],
                in0=scores[u][:],
                scalar=SCALING,
                in1=mask_sb[:, r, :],
                op0=ALU.mult,
                op1=ALU.add,
            )

        def negative_max(u):
            h = u % HEADS
            neg_max[u] = work.tile([P, 1], F32, name="neg_max")
            nc.vector.tensor_reduce(
                out=neg_max[u][:], in_=s_sb[h][:], axis=mybir.AxisListType.X, op=ALU.max, negate=True
            )

        def exponentials(u):
            r, h = divmod(u, HEADS)
            if h == 0:
                den[r] = per_round.tile([P, HEADS], F32, name="den")
            e_bf[u] = work.tile([P, SEQ + PAIR], BF16, name="e_bf")
            nc.scalar.activation(
                out=e_bf[u][:, 0 : SEQ + 1],
                in_=s_sb[h][:],
                func=ACT.Exp,
                bias=neg_max[u][:],
                scale=1.0,
                accum_out=den[r][:, h : h + 1],
            )

        def transpose_e(u):
            e_words = e_bf[u][:, 0:SEQ].bitcast(F32)
            e_flipped[u] = flip_banks.tile([P, HALVES, P], F32, name="e_flipped", tag="flipped")
            for j in range(HALVES):
                nc.tensor.transpose(e_flipped[u][:, j, :], e_words[:, j * P : (j + 1) * P], identity_f32[:])

        def group_e(u):
            e_grouped[u] = work.tile([P, P, HALVES], F32, name="e_grouped", align_bytes=64)
            nc.scalar.copy(out=e_grouped[u][:], in_=e_flipped[u][:].rearrange("p j q -> p q j"))

        def quantise_e(u):
            e_codes[u] = work.tile([P, P], U32, name="e_codes", align_bytes=64)
            e_scales[u] = work.tile([P, P], U8, name="e_scales", align_bytes=64)
            nc.vector.quantize_mx(
                out=e_codes[u][:].bitcast(FP8X4),
                scales=e_scales[u][:],
                in_=e_grouped[u][:].rearrange("p q j -> p (q j)").bitcast(BF16),
            )

        def multiply_ev(u):
            r, h = divmod(u, HEADS)
            g = h // GROUP
            if h == 0:
                product[r] = product_banks.tile([P, HEADS, HEAD_DIM], F32, name="product")
            nc.tensor.matmul_mx(
                out=product[r][:, h, :],
                lhsT=e_codes[u][:].bitcast(FP8X4),
                lhsT_scale=e_scales[u][:],
                rhs=v_codes[:, g, :].bitcast(FP8X4),
                rhs_scale=v_scales[:, g, :],
                start=True,
                stop=True,
            )

        def invert_den(r):
            inv_den[r] = per_round.tile([P, HEADS], F32, name="inv_den")
            nc.vector.reciprocal(out=inv_den[r][:], in_=den[r][:])

        def divide_and_store(u):
            r, h = divmod(u, HEADS)
            result = results.tile([P, HEAD_DIM], F32)
            nc.scalar.activation(
                out=result[:], in_=product[r][:, h, :], func=ACT.Copy, scale=inv_den[r][:, h : h + 1]
            )
            nc.sync.dma_start(out=out_dram[r, h], in_=result[:])

        transpose_rows(k_sb[0], kT[0], nc.vector.tensor_copy)
        transpose_rows(q_sb[0], qT[0], nc.scalar.copy)
        nc.vector.tensor_copy(out=v_grouped[:], in_=v_sb[:].rearrange("p g t d -> p g d t"))
        nc.vector.quantize_mx(
            out=v_codes[:].rearrange("p g d -> p (g d)").bitcast(FP8X4),
            scales=v_scales[:].rearrange("p g d -> p (g d)"),
            in_=v_grouped[:].rearrange("p g d t -> p (g d t)"),
        )
        transpose_rows(q_sb[1], qT[1], nc.scalar.copy)
        transpose_rows(k_sb[1], kT[1], nc.scalar.copy)
        transpose_rows(q_sb[2], qT[2], nc.scalar.copy)
        transpose_rows(q_sb[3], qT[3], nc.scalar.copy)

        for r in range(Q_TILES):
            for h in range(HEADS):
                u = r * HEADS + h
                multiply_qk(u)
                add_mask(u)
                negative_max(u)
                exponentials(u)
                transpose_e(u)
                group_e(u)
                quantise_e(u)
                multiply_ev(u)
            invert_den(r)
            for h in range(HEADS):
                divide_and_store(r * HEADS + h)
